import numpy as np
import ml_dtypes


BF16 = ml_dtypes.bfloat16


def bf(x):
    return np.asarray(x, np.float32).astype(BF16)


def f64(x):
    return np.asarray(x).astype(np.float64)


E2M1 = np.array([0.0, 0.5, 1.0, 1.5, 2.0, 3.0, 4.0, 6.0, -0.0, -0.5, -1.0, -1.5, -2.0, -3.0, -4.0, -6.0])


def pack_weight(w, fmt):
    k, n = w.shape
    w = f64(bf(w)).reshape(k // 32, 32, n)
    amax = np.abs(w).max(1)
    if fmt == "e4m3":
        byte = np.frexp(amax)[1] - 1 + 127 - 7
    else:
        mant, ex = np.frexp(amax / 6.0)
        byte = np.where(mant > 0.5, ex, ex - 1) + 127
    byte = np.clip(np.where(amax > 0, byte, 1), 1, 254)
    scaled = (w * np.exp2(127.0 - byte)[:, None, :]).reshape(k, n).astype(np.float32)
    by_word = np.ascontiguousarray(scaled.reshape(k // 512, 128, 4, n).transpose(0, 1, 3, 2))
    if fmt == "e4m3":
        words = by_word.astype(ml_dtypes.float8_e4m3fn).view(np.uint8)
    else:
        c = by_word.astype(ml_dtypes.float4_e2m1fn).view(np.uint8) & 0xF
        words = c[..., 0::2] | (c[..., 1::2] << 4)
    return np.ascontiguousarray(words), np.ascontiguousarray(byte.astype(np.uint8).reshape(k // 512, 16, n))


def unpack_weight(words, scales, fmt):
    g, p, n, _ = words.shape
    if fmt == "e4m3":
        vals = np.ascontiguousarray(words).view(ml_dtypes.float8_e4m3fn).astype(np.float64)
    else:
        nib = np.empty((g, p, n, 4), np.uint8)
        nib[..., 0::2] = words & 0xF
        nib[..., 1::2] = words >> 4
        vals = E2M1[nib]
    vals = vals * np.repeat(np.exp2(scales.astype(np.float64) - 127.0), 8, axis=1)[..., None]
    return vals.transpose(0, 1, 3, 2).reshape(g * 512, n)

def pack4(w):
    words, scales = pack_weight(w, "e2m1")
    return words.reshape(words.shape[0], 128, -1), scales


def unpack4(words, scales):
    return unpack_weight(words.reshape(words.shape[0], 128, -1, 2), scales, "e2m1")


def kspread(k):
    return np.exp2(np.repeat(np.random.randint(-6, 7, k // 32), 32).astype(np.float64))


B, T, C, H = 2, 64, 4096, 16
D = C // H
ROPE_BASE = 10000.0


def rope_cos_sin():
    inv_freq = 1.0 / (ROPE_BASE ** (np.arange(0, D, 2) / D))
    freqs = np.outer(np.arange(T) * 1.0, inv_freq)
    emb = np.concatenate([freqs, freqs], axis=-1)
    return np.cos(emb), np.sin(emb)


def rotate_half(v):
    v1, v2 = np.split(v, 2, axis=-1)
    return np.concatenate([-v2, v1], axis=-1)


def apply_rotary(v, cos, sin):
    return v * cos[None, None] + rotate_half(v) * sin[None, None]


def setup_inputs():
    s = kspread(C)
    x = np.random.standard_normal((B, T, C)) * s
    x_words, x_scales = pack4(x.reshape(B * T, C).T)
    words, scales = pack4(np.random.standard_normal((C, 2 * C)) / np.sqrt(C) / s[:, None])
    b_qk = bf(np.random.standard_normal(2 * C) * 0.3)
    return {"x_words": x_words, "x_scales": x_scales, "W_qk_words": words, "W_qk_scales": scales, "b_qk": b_qk}


def reference(x_words, x_scales, W_qk_words, W_qk_scales, b_qk):
    xq = unpack4(x_words, x_scales).T.reshape(B, T, C)
    qk = (xq @ unpack4(W_qk_words, W_qk_scales)) + f64(b_qk)
    q, k = np.split(qk, 2, axis=2)
    q = q.reshape(B, T, H, D).transpose(0, 2, 1, 3)
    k = k.reshape(B, T, H, D).transpose(0, 2, 1, 3)
    cos, sin = rope_cos_sin()
    return apply_rotary(q, cos, sin), apply_rotary(k, cos, sin)

@@ -1,0 +1,208 @@
+from contextlib import ExitStack
+
+import concourse.mybir as mybir
+from concourse.masks import make_identity
+
+F32 = mybir.dt.float32
+BF16 = mybir.dt.bfloat16
+I32 = mybir.dt.int32
+U8 = mybir.dt.uint8
+FP4X4 = mybir.dt.float4_e2m1fn_x4
+ALU = mybir.AluOpType
+ACT = mybir.ActivationFunctionType
+
+P = 128
+PASSES = 8
+TOKENS = 128
+HEADS = 16
+HEAD_DIM = 256
+HALF = 128
+COLS = 8192
+BANK = 512
+GROUP_COLS = 2048
+LN_ROPE_BASE = 9.210340371976184
+PI = 3.141592653589793
+
+FLOPS = 2 * TOKENS * 4096 * COLS
+
+CHUNK_BANKS = [4, 4, 4, 2, 2]
+RESIDENT_CHUNKS = 3
+
+
+def tile_causalselfattention_pa_kernel(tc, x_words, x_scales, W_qk_words, W_qk_scales, b_qk, out_0, out_1):
+    nc = tc.nc
+    with ExitStack() as ctx:
+        keep = ctx.enter_context(tc.tile_pool(name="keep", bufs=1))
+        wpool = ctx.enter_context(tc.tile_pool(name="wpool", bufs=24))
+        work = ctx.enter_context(tc.tile_pool(name="work", bufs=2))
+        outp = ctx.enter_context(tc.tile_pool(name="outp", bufs=16))
+        psum = ctx.enter_context(tc.psum_pool(name="psum", bufs=8))
+        ctx.enter_context(tc.manual_schedule())
+
+        x_raw = keep.tile([P, PASSES, 2 * TOKENS], U8, name="x_raw", align_bytes=64)
+        x_codes = keep.tile([P, PASSES, 2 * TOKENS], U8, name="x_codes", align_bytes=64)
+        xs_raw = keep.tile([P, PASSES, TOKENS], U8, name="xs_raw", align_bytes=64)
+        x_plane = keep.tile([P, PASSES, TOKENS], U8, name="x_plane", align_bytes=64)
+        planes = []
+        for s in range(COLS // GROUP_COLS):
+            pl = keep.tile([P, PASSES, GROUP_COLS], U8, name="plane%d" % s, align_bytes=64)
+            planes.append(pl)
+        bias_all = keep.tile([P, COLS], BF16, name="bias_all")
+        bias_rows = keep.tile([P, BANK], BF16, name="bias_rows")
+        ident = keep.tile([P, P], BF16, name="ident")
+        cos_t = keep.tile([P, BANK], F32, name="cos_t")
+        sin_t = keep.tile([P, BANK], F32, name="sin_t")
+        col_i = keep.tile([P, HALF], I32, name="col_i")
+        row_i = keep.tile([P, 1], I32, name="row_i")
+
+        nc.vector.memset(xs_raw[:].bitcast(I32), 0)
+        nc.vector.memset(planes[0][:].bitcast(I32), 0)
+        nc.gpsimd.memset(bias_rows[:], 0.0)
+        nc.gpsimd.iota(col_i[:], pattern=[[1, HALF]], base=0, channel_multiplier=0)
+        nc.gpsimd.iota(row_i[:], pattern=[[0, 1]], base=0, channel_multiplier=1)
+        make_identity(nc, ident[:])
+        for s in range(1, COLS // GROUP_COLS):
+            nc.gpsimd.memset(planes[s][:].bitcast(F32), 0.0)
+
+        def load_scale_rows(plane, src):
+            for r in range(4):
+                nc.sync.dma_start(
+                    out=plane[r:P:32, :, :].bitcast(I32),
+                    in_=src[:, r:16:4, :].rearrange("g q n -> q g n").bitcast(I32),
+                )
+
+        def load_group_scales(s):
+            load_scale_rows(planes[s], W_qk_scales[:, :, s * GROUP_COLS:(s + 1) * GROUP_COLS])
+
+        starts = []
+        c0 = 0
+        for nb in CHUNK_BANKS:
+            starts.append(c0)
+            c0 += nb * BANK
+
+        chunk_tiles = {}
+
+        def load_codes(c, first, count):
+            nb = CHUNK_BANKS[c]
+            ng = 4 // nb
+            for k in range(first, first + count):
+                t = wpool.tile([P, ng, nb * 2 * BANK], U8, name="wc", tag="wc", align_bytes=64)
+                nc.sync.dma_start(
+                    out=t[:].bitcast(I32),
+                    in_=W_qk_words[k * ng:(k + 1) * ng, :, 2 * starts[c]:2 * (starts[c] + nb * BANK)].rearrange("g p n -> p g n").bitcast(I32),
+                )
+                for i in range(ng):
+                    chunk_tiles[(c, k * ng + i)] = (t, i)
+
+        nc.scalar.dma_start(out=bias_rows[0:16, :], in_=b_qk.rearrange("(n c) -> n c", c=BANK))
+        nc.sync.dma_start(out=x_raw[:].bitcast(I32), in_=x_words.rearrange("g p n -> p g n").bitcast(I32))
+        load_scale_rows(xs_raw, x_scales)
+        load_codes(0, 0, 2)
+        load_group_scales(0)
+        load_codes(0, 2, 6)
+        load_group_scales(1)
+        load_codes(1, 0, 8)
+        load_group_scales(2)
+        load_codes(2, 0, 8)
+        load_group_scales(3)
+
+        col_f = keep.tile([P, HALF], F32, name="col_f")
+        nc.vector.tensor_copy(out=col_f[:], in_=col_i[:])
+        pos_i = keep.tile([P, 1], I32, name="pos_i")
+        nc.vector.tensor_single_scalar(out=pos_i[:], in_=row_i[:], scalar=1, op=ALU.arith_shift_right)
+        pos_f = keep.tile([P, 1], F32, name="pos_f")
+        nc.vector.tensor_copy(out=pos_f[:], in_=pos_i[:])
+        freq = keep.tile([P, HALF], F32, name="freq")
+        nc.scalar.activation(out=freq[:], in_=col_f[:], func=ACT.Exp, scale=-LN_ROPE_BASE / HALF)
+
+        for g in range(PASSES):
+            nc.vector.tensor_copy(
+                out=x_codes[:, g, :].rearrange("p (t b e) -> p t b e", b=2, e=2),
+                in_=x_raw[:, g, :].rearrange("p (b t e) -> p t b e", b=2, e=2),
+            )
+        nc.vector.tensor_copy(
+            out=x_plane[:].rearrange("p g (t b) -> p g t b", b=2),
+            in_=xs_raw[:].rearrange("p g (b t) -> p g t b", b=2),
+        )
+
+        ang = keep.tile([P, 2 * HALF], F32, name="ang")
+        nc.vector.tensor_scalar(out=ang[:, 0:HALF], in0=freq[:], scalar1=pos_f[:, 0:1], scalar2=None, op0=ALU.mult)
+        nc.vector.tensor_scalar(out=ang[:, HALF:2 * HALF], in0=freq[:], scalar1=pos_f[:, 0:1], scalar2=0.5 * PI, op0=ALU.mult, op1=ALU.add)
+        turns_i = keep.tile([P, 2 * HALF], I32, name="turns_i")
+        nc.vector.tensor_scalar(out=turns_i[:], in0=ang[:], scalar1=0.5 / PI, scalar2=None, op0=ALU.mult)
+        turns = keep.tile([P, 2 * HALF], F32, name="turns")
+        nc.vector.tensor_copy(out=turns[:], in_=turns_i[:])
+        big = 6.28125
+        small = 2.0 * PI - big
+        flag = keep.tile([P, 2 * HALF], F32, name="flag")
+        nc.vector.scalar_tensor_tensor(out=ang[:], in0=turns[:], scalar=-big, in1=ang[:], op0=ALU.mult, op1=ALU.add)
+        nc.vector.scalar_tensor_tensor(out=ang[:], in0=turns[:], scalar=-small, in1=ang[:], op0=ALU.mult, op1=ALU.add)
+        nc.vector.tensor_scalar(out=flag[:], in0=ang[:], scalar1=PI, scalar2=None, op0=ALU.is_gt)
+        nc.vector.scalar_tensor_tensor(out=ang[:], in0=flag[:], scalar=-2.0 * PI, in1=ang[:], op0=ALU.mult, op1=ALU.add)
+        nc.vector.tensor_scalar(out=flag[:], in0=ang[:], scalar1=-PI, scalar2=None, op0=ALU.is_lt)
+        nc.vector.scalar_tensor_tensor(out=ang[:], in0=flag[:], scalar=2.0 * PI, in1=ang[:], op0=ALU.mult, op1=ALU.add)
+
+        for n in range(COLS // BANK):
+            pb = psum.tile([P, BANK], F32, name="acc", tag="acc")
+            nc.tensor.matmul(out=pb[:], lhsT=ident[:, n:n + 1].to_broadcast([P, P]), rhs=bias_rows[:], start=True, stop=True)
+            nc.scalar.copy(out=bias_all[:, n * BANK:(n + 1) * BANK], in_=pb[:])
+
+        for i in range(4):
+            nc.scalar.activation(out=cos_t[:, i * HALF:(i + 1) * HALF], in_=ang[:, HALF:2 * HALF], func=ACT.Sin)
+            nc.scalar.activation(out=sin_t[:, i * HALF:(i + 1) * HALF], in_=ang[:, 0:HALF], func=ACT.Sin, scale=(1.0 if i % 2 == 0 else -1.0))
+
+        def multiply(c):
+            nb = CHUNK_BANKS[c]
+            accs = []
+            for j in range(nb):
+                acc = psum.tile([P, BANK], F32, name="acc", tag="acc")
+                accs.append(acc)
+            plane = planes[starts[c] // GROUP_COLS]
+            off = starts[c] % GROUP_COLS
+            for g in range(PASSES):
+                t, i = chunk_tiles[(c, g)]
+                for j in range(nb):
+                    nc.tensor.matmul_mx(
+                        out=accs[j][:],
+                        lhsT=x_codes[:, g, :].bitcast(FP4X4),
+                        lhsT_scale=x_plane[:, g, :],
+                        rhs=t[:, i, j * 2 * BANK:(j + 1) * 2 * BANK].bitcast(FP4X4),
+                        rhs_scale=plane[:, g, off + j * BANK:off + (j + 1) * BANK],
+                        start=(g == 0),
+                        stop=(g == PASSES - 1),
+                    )
+            return accs
+
+        def rotate(parts):
+            vs = []
+            for acc, col in parts:
+                v = work.tile([P, BANK], F32, name="v", tag="v")
+                nc.vector.tensor_tensor(out=v[:], in0=acc[:], in1=bias_all[:, col:col + BANK], op=ALU.add)
+                vs.append(v)
+            prods = []
+            for v in vs:
+                a = outp.tile([P, BANK], F32, name="a", tag="a")
+                b = work.tile([P, BANK], F32, name="b", tag="b")
+                nc.vector.tensor_tensor(out=a[:], in0=v[:], in1=cos_t[:], op=ALU.mult)
+                nc.vector.tensor_tensor(out=b[:], in0=v[:], in1=sin_t[:], op=ALU.mult)
+                prods.append((a, b))
+            for (acc, col), (a, b) in zip(parts, prods):
+                a4 = a[:].rearrange("p (h s j) -> p h s j", s=2, j=HALF)
+                b4 = b[:].rearrange("p (h s j) -> p h s j", s=2, j=HALF)
+                nc.vector.tensor_tensor(out=a4[:, :, 0, :], in0=a4[:, :, 0, :], in1=b4[:, :, 1, :], op=ALU.add)
+                nc.vector.tensor_tensor(out=a4[:, :, 1, :], in0=a4[:, :, 1, :], in1=b4[:, :, 0, :], op=ALU.add)
+                for hh in range(BANK // HEAD_DIM):
+                    head = col // HEAD_DIM + hh
+                    dst = out_0 if head < HEADS else out_1
+                    nc.sync.dma_start(
+                        out=dst[:, head % HEADS, :, :].rearrange("b t d -> t b d"),
+                        in_=a[:, hh * HEAD_DIM:(hh + 1) * HEAD_DIM],
+                    )
+
+        for c in range(len(CHUNK_BANKS)):
+            accs = multiply(c)
+            if c == 0:
+                for k in range(RESIDENT_CHUNKS, len(CHUNK_BANKS)):
+                    load_codes(k, 0, PASSES * CHUNK_BANKS[k] // 4)
+            for j in range(0, CHUNK_BANKS[c], 2):
+                rotate([(accs[j], starts[c] + j * BANK), (accs[j + 1], starts[c] + (j + 1) * BANK)])

@@ -33,9 +33,9 @@ def tile_causalselfattention_pa_kernel(tc, x_words, x_scales, W_qk_words, W_qk_s
     nc = tc.nc
     with ExitStack() as ctx:
         keep = ctx.enter_context(tc.tile_pool(name="keep", bufs=1))
-        wpool = ctx.enter_context(tc.tile_pool(name="wpool", bufs=24))
+        wpool = ctx.enter_context(tc.tile_pool(name="wpool", bufs=12))
         work = ctx.enter_context(tc.tile_pool(name="work", bufs=2))
-        outp = ctx.enter_context(tc.tile_pool(name="outp", bufs=16))
+        outp = ctx.enter_context(tc.tile_pool(name="outp", bufs=1))
         psum = ctx.enter_context(tc.psum_pool(name="psum", bufs=8))
         ctx.enter_context(tc.manual_schedule())
 
@@ -84,7 +84,7 @@ def tile_causalselfattention_pa_kernel(tc, x_words, x_scales, W_qk_words, W_qk_s
 
         def load_codes(c, first, count):
             nb = CHUNK_BANKS[c]
-            ng = 4 // nb
+            ng = 8 // nb
             for k in range(first, first + count):
                 t = wpool.tile([P, ng, nb * 2 * BANK], U8, name="wc", tag="wc", align_bytes=64)
                 nc.sync.dma_start(
@@ -97,13 +97,13 @@ def tile_causalselfattention_pa_kernel(tc, x_words, x_scales, W_qk_words, W_qk_s
         nc.scalar.dma_start(out=bias_rows[0:16, :], in_=b_qk.rearrange("(n c) -> n c", c=BANK))
         nc.sync.dma_start(out=x_raw[:].bitcast(I32), in_=x_words.rearrange("g p n -> p g n").bitcast(I32))
         load_scale_rows(xs_raw, x_scales)
-        load_codes(0, 0, 2)
+        load_codes(0, 0, 1)
         load_group_scales(0)
-        load_codes(0, 2, 6)
+        load_codes(0, 1, 3)
         load_group_scales(1)
-        load_codes(1, 0, 8)
+        load_codes(1, 0, 4)
         load_group_scales(2)
-        load_codes(2, 0, 8)
+        load_codes(2, 0, 4)
         load_group_scales(3)
 
         col_f = keep.tile([P, HALF], F32, name="col_f")
@@ -175,34 +175,36 @@ def tile_causalselfattention_pa_kernel(tc, x_words, x_scales, W_qk_words, W_qk_s
 
         def rotate(parts):
             vs = []
-            for acc, col in parts:
+            for acc, col, a in parts:
                 v = work.tile([P, BANK], F32, name="v", tag="v")
                 nc.vector.tensor_tensor(out=v[:], in0=acc[:], in1=bias_all[:, col:col + BANK], op=ALU.add)
                 vs.append(v)
             prods = []
-            for v in vs:
-                a = outp.tile([P, BANK], F32, name="a", tag="a")
+            for (acc, col, a), v in zip(parts, vs):
                 b = work.tile([P, BANK], F32, name="b", tag="b")
-                nc.vector.tensor_tensor(out=a[:], in0=v[:], in1=cos_t[:], op=ALU.mult)
+                nc.vector.tensor_tensor(out=a, in0=v[:], in1=cos_t[:], op=ALU.mult)
                 nc.vector.tensor_tensor(out=b[:], in0=v[:], in1=sin_t[:], op=ALU.mult)
-                prods.append((a, b))
-            for (acc, col), (a, b) in zip(parts, prods):
-                a4 = a[:].rearrange("p (h s j) -> p h s j", s=2, j=HALF)
+                prods.append(b)
+            for (acc, col, a), b in zip(parts, prods):
+                a4 = a.rearrange("p (h s j) -> p h s j", s=2, j=HALF)
                 b4 = b[:].rearrange("p (h s j) -> p h s j", s=2, j=HALF)
                 nc.vector.tensor_tensor(out=a4[:, :, 0, :], in0=a4[:, :, 0, :], in1=b4[:, :, 1, :], op=ALU.add)
                 nc.vector.tensor_tensor(out=a4[:, :, 1, :], in0=a4[:, :, 1, :], in1=b4[:, :, 0, :], op=ALU.add)
-                for hh in range(BANK // HEAD_DIM):
-                    head = col // HEAD_DIM + hh
-                    dst = out_0 if head < HEADS else out_1
-                    nc.sync.dma_start(
-                        out=dst[:, head % HEADS, :, :].rearrange("b t d -> t b d"),
-                        in_=a[:, hh * HEAD_DIM:(hh + 1) * HEAD_DIM],
-                    )
 
         for c in range(len(CHUNK_BANKS)):
             accs = multiply(c)
             if c == 0:
                 for k in range(RESIDENT_CHUNKS, len(CHUNK_BANKS)):
-                    load_codes(k, 0, PASSES * CHUNK_BANKS[k] // 4)
-            for j in range(0, CHUNK_BANKS[c], 2):
-                rotate([(accs[j], starts[c] + j * BANK), (accs[j + 1], starts[c] + (j + 1) * BANK)])
+                    load_codes(k, 0, PASSES * CHUNK_BANKS[k] // 8)
+            nb = CHUNK_BANKS[c]
+            o = outp.tile([P, nb * BANK], F32, name="o%d" % c)
+            for j in range(0, nb, 2):
+                rotate([(accs[i], starts[c] + i * BANK, o[:, i * BANK:(i + 1) * BANK]) for i in (j, j + 1)])
+            head = starts[c] // HEAD_DIM
+            dst = out_0 if head < HEADS else out_1
+            h0 = head % HEADS
+            for b in range(2):
+                nc.sync.dma_start(
+                    out=dst[b, h0:h0 + nb * BANK // HEAD_DIM, :, :].rearrange("h t d -> t h d"),
+                    in_=o[b:P:2, :].rearrange("p (h d) -> p h d", d=HEAD_DIM),
+                )

@@ -33,9 +33,9 @@ def tile_causalselfattention_pa_kernel(tc, x_words, x_scales, W_qk_words, W_qk_s
     nc = tc.nc
     with ExitStack() as ctx:
         keep = ctx.enter_context(tc.tile_pool(name="keep", bufs=1))
-        wpool = ctx.enter_context(tc.tile_pool(name="wpool", bufs=12))
+        wpool = ctx.enter_context(tc.tile_pool(name="wpool", bufs=24))
         work = ctx.enter_context(tc.tile_pool(name="work", bufs=2))
-        outp = ctx.enter_context(tc.tile_pool(name="outp", bufs=1))
+        outp = ctx.enter_context(tc.tile_pool(name="outp", bufs=16))
         psum = ctx.enter_context(tc.psum_pool(name="psum", bufs=8))
         ctx.enter_context(tc.manual_schedule())
 
@@ -84,7 +84,7 @@ def tile_causalselfattention_pa_kernel(tc, x_words, x_scales, W_qk_words, W_qk_s
 
         def load_codes(c, first, count):
             nb = CHUNK_BANKS[c]
-            ng = 8 // nb
+            ng = 4 // nb
             for k in range(first, first + count):
                 t = wpool.tile([P, ng, nb * 2 * BANK], U8, name="wc", tag="wc", align_bytes=64)
                 nc.sync.dma_start(
@@ -97,14 +97,13 @@ def tile_causalselfattention_pa_kernel(tc, x_words, x_scales, W_qk_words, W_qk_s
         nc.scalar.dma_start(out=bias_rows[0:16, :], in_=b_qk.rearrange("(n c) -> n c", c=BANK))
         nc.sync.dma_start(out=x_raw[:].bitcast(I32), in_=x_words.rearrange("g p n -> p g n").bitcast(I32))
         load_scale_rows(xs_raw, x_scales)
-        load_codes(0, 0, 1)
         load_group_scales(0)
-        load_codes(0, 1, 3)
         load_group_scales(1)
-        load_codes(1, 0, 4)
         load_group_scales(2)
-        load_codes(2, 0, 4)
         load_group_scales(3)
+        load_codes(0, 0, 8)
+        load_codes(1, 0, 8)
+        load_codes(2, 0, 8)
 
         col_f = keep.tile([P, HALF], F32, name="col_f")
         nc.vector.tensor_copy(out=col_f[:], in_=col_i[:])
@@ -175,36 +174,34 @@ def tile_causalselfattention_pa_kernel(tc, x_words, x_scales, W_qk_words, W_qk_s
 
         def rotate(parts):
             vs = []
-            for acc, col, a in parts:
+            for acc, col in parts:
                 v = work.tile([P, BANK], F32, name="v", tag="v")
                 nc.vector.tensor_tensor(out=v[:], in0=acc[:], in1=bias_all[:, col:col + BANK], op=ALU.add)
                 vs.append(v)
             prods = []
-            for (acc, col, a), v in zip(parts, vs):
+            for v in vs:
+                a = outp.tile([P, BANK], F32, name="a", tag="a")
                 b = work.tile([P, BANK], F32, name="b", tag="b")
-                nc.vector.tensor_tensor(out=a, in0=v[:], in1=cos_t[:], op=ALU.mult)
+                nc.vector.tensor_tensor(out=a[:], in0=v[:], in1=cos_t[:], op=ALU.mult)
                 nc.vector.tensor_tensor(out=b[:], in0=v[:], in1=sin_t[:], op=ALU.mult)
-                prods.append(b)
-            for (acc, col, a), b in zip(parts, prods):
-                a4 = a.rearrange("p (h s j) -> p h s j", s=2, j=HALF)
+                prods.append((a, b))
+            for (acc, col), (a, b) in zip(parts, prods):
+                a4 = a[:].rearrange("p (h s j) -> p h s j", s=2, j=HALF)
                 b4 = b[:].rearrange("p (h s j) -> p h s j", s=2, j=HALF)
                 nc.vector.tensor_tensor(out=a4[:, :, 0, :], in0=a4[:, :, 0, :], in1=b4[:, :, 1, :], op=ALU.add)
                 nc.vector.tensor_tensor(out=a4[:, :, 1, :], in0=a4[:, :, 1, :], in1=b4[:, :, 0, :], op=ALU.add)
+                for hh in range(BANK // HEAD_DIM):
+                    head = col // HEAD_DIM + hh
+                    dst = out_0 if head < HEADS else out_1
+                    nc.sync.dma_start(
+                        out=dst[:, head % HEADS, :, :].rearrange("b t d -> t b d"),
+                        in_=a[:, hh * HEAD_DIM:(hh + 1) * HEAD_DIM],
+                    )
 
         for c in range(len(CHUNK_BANKS)):
             accs = multiply(c)
             if c == 0:
                 for k in range(RESIDENT_CHUNKS, len(CHUNK_BANKS)):
-                    load_codes(k, 0, PASSES * CHUNK_BANKS[k] // 8)
-            nb = CHUNK_BANKS[c]
-            o = outp.tile([P, nb * BANK], F32, name="o%d" % c)
-            for j in range(0, nb, 2):
-                rotate([(accs[i], starts[c] + i * BANK, o[:, i * BANK:(i + 1) * BANK]) for i in (j, j + 1)])
-            head = starts[c] // HEAD_DIM
-            dst = out_0 if head < HEADS else out_1
-            h0 = head % HEADS
-            for b in range(2):
-                nc.sync.dma_start(
-                    out=dst[b, h0:h0 + nb * BANK // HEAD_DIM, :, :].rearrange("h t d -> t h d"),
-                    in_=o[b:P:2, :].rearrange("p (h d) -> p h d", d=HEAD_DIM),
-                )
+                    load_codes(k, 0, PASSES * CHUNK_BANKS[k] // 4)
+            for j in range(0, CHUNK_BANKS[c], 2):
+                rotate([(accs[j], starts[c] + j * BANK), (accs[j + 1], starts[c] + (j + 1) * BANK)])

@@ -44,8 +44,8 @@ def tile_causalselfattention_pa_kernel(tc, x_words, x_scales, W_qk_words, W_qk_s
         xs_raw = keep.tile([P, PASSES, TOKENS], U8, name="xs_raw", align_bytes=64)
         x_plane = keep.tile([P, PASSES, TOKENS], U8, name="x_plane", align_bytes=64)
         planes = []
-        for s in range(COLS // GROUP_COLS):
-            pl = keep.tile([P, PASSES, GROUP_COLS], U8, name="plane%d" % s, align_bytes=64)
+        for g in range(PASSES):
+            pl = keep.tile([P, COLS], U8, name="plane%d" % g, align_bytes=64)
             planes.append(pl)
         bias_all = keep.tile([P, COLS], BF16, name="bias_all")
         bias_rows = keep.tile([P, BANK], BF16, name="bias_rows")
@@ -55,14 +55,15 @@ def tile_causalselfattention_pa_kernel(tc, x_words, x_scales, W_qk_words, W_qk_s
         col_i = keep.tile([P, HALF], I32, name="col_i")
         row_i = keep.tile([P, 1], I32, name="row_i")
 
+        for g in range(PASSES // 2):
+            nc.vector.memset(planes[g][:].bitcast(I32), 0)
         nc.vector.memset(xs_raw[:].bitcast(I32), 0)
-        nc.vector.memset(planes[0][:].bitcast(I32), 0)
         nc.gpsimd.memset(bias_rows[:], 0.0)
         nc.gpsimd.iota(col_i[:], pattern=[[1, HALF]], base=0, channel_multiplier=0)
         nc.gpsimd.iota(row_i[:], pattern=[[0, 1]], base=0, channel_multiplier=1)
         make_identity(nc, ident[:])
-        for s in range(1, COLS // GROUP_COLS):
-            nc.gpsimd.memset(planes[s][:].bitcast(F32), 0.0)
+        for g in range(PASSES // 2, PASSES):
+            nc.gpsimd.memset(planes[g][:].bitcast(F32), 0.0)
 
         def load_scale_rows(plane, src):
             for r in range(4):
@@ -71,8 +72,12 @@ def tile_causalselfattention_pa_kernel(tc, x_words, x_scales, W_qk_words, W_qk_s
                     in_=src[:, r:16:4, :].rearrange("g q n -> q g n").bitcast(I32),
                 )
 
-        def load_group_scales(s):
-            load_scale_rows(planes[s], W_qk_scales[:, :, s * GROUP_COLS:(s + 1) * GROUP_COLS])
+        def load_pass_scales(g):
+            for r in range(4):
+                nc.sync.dma_start(
+                    out=planes[g][r:P:32, :].bitcast(I32),
+                    in_=W_qk_scales[g, r:16:4, :].bitcast(I32),
+                )
 
         starts = []
         c0 = 0
@@ -96,11 +101,9 @@ def tile_causalselfattention_pa_kernel(tc, x_words, x_scales, W_qk_words, W_qk_s
 
         nc.scalar.dma_start(out=bias_rows[0:16, :], in_=b_qk.rearrange("(n c) -> n c", c=BANK))
         nc.sync.dma_start(out=x_raw[:].bitcast(I32), in_=x_words.rearrange("g p n -> p g n").bitcast(I32))
+        for g in range(PASSES):
+            load_pass_scales(g)
         load_scale_rows(xs_raw, x_scales)
-        load_group_scales(0)
-        load_group_scales(1)
-        load_group_scales(2)
-        load_group_scales(3)
         load_codes(0, 0, 8)
         load_codes(1, 0, 8)
         load_codes(2, 0, 8)
@@ -119,10 +122,6 @@ def tile_causalselfattention_pa_kernel(tc, x_words, x_scales, W_qk_words, W_qk_s
                 out=x_codes[:, g, :].rearrange("p (t b e) -> p t b e", b=2, e=2),
                 in_=x_raw[:, g, :].rearrange("p (b t e) -> p t b e", b=2, e=2),
             )
-        nc.vector.tensor_copy(
-            out=x_plane[:].rearrange("p g (t b) -> p g t b", b=2),
-            in_=xs_raw[:].rearrange("p g (b t) -> p g t b", b=2),
-        )
 
         ang = keep.tile([P, 2 * HALF], F32, name="ang")
         nc.vector.tensor_scalar(out=ang[:, 0:HALF], in0=freq[:], scalar1=pos_f[:, 0:1], scalar2=None, op0=ALU.mult)
@@ -141,6 +140,11 @@ def tile_causalselfattention_pa_kernel(tc, x_words, x_scales, W_qk_words, W_qk_s
         nc.vector.tensor_scalar(out=flag[:], in0=ang[:], scalar1=-PI, scalar2=None, op0=ALU.is_lt)
         nc.vector.scalar_tensor_tensor(out=ang[:], in0=flag[:], scalar=2.0 * PI, in1=ang[:], op0=ALU.mult, op1=ALU.add)
 
+        nc.vector.tensor_copy(
+            out=x_plane[:].rearrange("p g (t b) -> p g t b", b=2),
+            in_=xs_raw[:].rearrange("p g (b t) -> p g t b", b=2),
+        )
+
         for n in range(COLS // BANK):
             pb = psum.tile([P, BANK], F32, name="acc", tag="acc")
             nc.tensor.matmul(out=pb[:], lhsT=ident[:, n:n + 1].to_broadcast([P, P]), rhs=bias_rows[:], start=True, stop=True)
@@ -156,8 +160,7 @@ def tile_causalselfattention_pa_kernel(tc, x_words, x_scales, W_qk_words, W_qk_s
             for j in range(nb):
                 acc = psum.tile([P, BANK], F32, name="acc", tag="acc")
                 accs.append(acc)
-            plane = planes[starts[c] // GROUP_COLS]
-            off = starts[c] % GROUP_COLS
+            off = starts[c]
             for g in range(PASSES):
                 t, i = chunk_tiles[(c, g)]
                 for j in range(nb):
@@ -166,7 +169,7 @@ def tile_causalselfattention_pa_kernel(tc, x_words, x_scales, W_qk_words, W_qk_s
                         lhsT=x_codes[:, g, :].bitcast(FP4X4),
                         lhsT_scale=x_plane[:, g, :],
                         rhs=t[:, i, j * 2 * BANK:(j + 1) * 2 * BANK].bitcast(FP4X4),
-                        rhs_scale=plane[:, g, off + j * BANK:off + (j + 1) * BANK],
+                        rhs_scale=planes[g][:, off + j * BANK:off + (j + 1) * BANK],
                         start=(g == 0),
                         stop=(g == PASSES - 1),
                     )

@@ -44,8 +44,8 @@ def tile_causalselfattention_pa_kernel(tc, x_words, x_scales, W_qk_words, W_qk_s
         xs_raw = keep.tile([P, PASSES, TOKENS], U8, name="xs_raw", align_bytes=64)
         x_plane = keep.tile([P, PASSES, TOKENS], U8, name="x_plane", align_bytes=64)
         planes = []
-        for g in range(PASSES):
-            pl = keep.tile([P, COLS], U8, name="plane%d" % g, align_bytes=64)
+        for s in range(PASSES // 2):
+            pl = keep.tile([P, 2, COLS], U8, name="plane%d" % s, align_bytes=64)
             planes.append(pl)
         bias_all = keep.tile([P, COLS], BF16, name="bias_all")
         bias_rows = keep.tile([P, BANK], BF16, name="bias_rows")
@@ -55,15 +55,15 @@ def tile_causalselfattention_pa_kernel(tc, x_words, x_scales, W_qk_words, W_qk_s
         col_i = keep.tile([P, HALF], I32, name="col_i")
         row_i = keep.tile([P, 1], I32, name="row_i")
 
-        for g in range(PASSES // 2):
-            nc.vector.memset(planes[g][:].bitcast(I32), 0)
+        nc.vector.memset(planes[0][:].bitcast(I32), 0)
+        nc.vector.memset(planes[1][:].bitcast(I32), 0)
         nc.vector.memset(xs_raw[:].bitcast(I32), 0)
         nc.gpsimd.memset(bias_rows[:], 0.0)
         nc.gpsimd.iota(col_i[:], pattern=[[1, HALF]], base=0, channel_multiplier=0)
         nc.gpsimd.iota(row_i[:], pattern=[[0, 1]], base=0, channel_multiplier=1)
         make_identity(nc, ident[:])
-        for g in range(PASSES // 2, PASSES):
-            nc.gpsimd.memset(planes[g][:].bitcast(F32), 0.0)
+        for s in range(2, PASSES // 2):
+            nc.gpsimd.memset(planes[s][:].bitcast(F32), 0.0)
 
         def load_scale_rows(plane, src):
             for r in range(4):
@@ -72,11 +72,12 @@ def tile_causalselfattention_pa_kernel(tc, x_words, x_scales, W_qk_words, W_qk_s
                     in_=src[:, r:16:4, :].rearrange("g q n -> q g n").bitcast(I32),
                 )
 
-        def load_pass_scales(g):
-            for r in range(4):
+        def load_group_scales(s):
+            for p in (0, 1, 2, 3, 32, 33, 34, 35):
+                q = 4 * (p // 32) + p % 32
                 nc.sync.dma_start(
-                    out=planes[g][r:P:32, :].bitcast(I32),
-                    in_=W_qk_scales[g, r:16:4, :].bitcast(I32),
+                    out=planes[s][p:P:64, :, :].bitcast(I32),
+                    in_=W_qk_scales[2 * s:2 * s + 2, q:16:8, :].rearrange("g q n -> q g n").bitcast(I32),
                 )
 
         starts = []
@@ -101,8 +102,10 @@ def tile_causalselfattention_pa_kernel(tc, x_words, x_scales, W_qk_words, W_qk_s
 
         nc.scalar.dma_start(out=bias_rows[0:16, :], in_=b_qk.rearrange("(n c) -> n c", c=BANK))
         nc.sync.dma_start(out=x_raw[:].bitcast(I32), in_=x_words.rearrange("g p n -> p g n").bitcast(I32))
-        for g in range(PASSES):
-            load_pass_scales(g)
+        load_group_scales(0)
+        load_group_scales(1)
+        load_group_scales(2)
+        load_group_scales(3)
         load_scale_rows(xs_raw, x_scales)
         load_codes(0, 0, 8)
         load_codes(1, 0, 8)
@@ -169,7 +172,7 @@ def tile_causalselfattention_pa_kernel(tc, x_words, x_scales, W_qk_words, W_qk_s
                         lhsT=x_codes[:, g, :].bitcast(FP4X4),
                         lhsT_scale=x_plane[:, g, :],
                         rhs=t[:, i, j * 2 * BANK:(j + 1) * 2 * BANK].bitcast(FP4X4),
-                        rhs_scale=planes[g][:, off + j * BANK:off + (j + 1) * BANK],
+                        rhs_scale=planes[g // 2][:, g % 2, off + j * BANK:off + (j + 1) * BANK],
                         start=(g == 0),
                         stop=(g == PASSES - 1),
                     )

@@ -36,12 +36,17 @@ def tile_causalselfattention_pa_kernel(tc, x_words, x_scales, W_qk_words, W_qk_s
         wpool = ctx.enter_context(tc.tile_pool(name="wpool", bufs=24))
         work = ctx.enter_context(tc.tile_pool(name="work", bufs=2))
         outp = ctx.enter_context(tc.tile_pool(name="outp", bufs=16))
-        psum = ctx.enter_context(tc.psum_pool(name="psum", bufs=8))
+        ptab = ctx.enter_context(tc.psum_pool(name="ptab", bufs=1))
+        psum = ctx.enter_context(tc.psum_pool(name="psum", bufs=7))
         ctx.enter_context(tc.manual_schedule())
 
-        x_raw = keep.tile([P, PASSES, 2 * TOKENS], U8, name="x_raw", align_bytes=64)
+        scr_f = work.tile([P, 2 * BANK], F32, name="scr_f", tag="u")
+        scr_i = work.tile([P, 2 * BANK], I32, name="scr_i", tag="u")
+        scr_t = work.tile([P, 2 * BANK], F32, name="scr_t", tag="bsw")
+        scr_x = work.tile([P, 8 * BANK], U8, name="scr_x", tag="bsw")
+        x_raw = scr_x[:, 0:PASSES * 2 * TOKENS].rearrange("p (g n) -> p g n", g=PASSES)
+        xs_raw = scr_x[:, PASSES * 2 * TOKENS:PASSES * 3 * TOKENS].rearrange("p (g n) -> p g n", g=PASSES)
         x_codes = keep.tile([P, PASSES, 2 * TOKENS], U8, name="x_codes", align_bytes=64)
-        xs_raw = keep.tile([P, PASSES, TOKENS], U8, name="xs_raw", align_bytes=64)
         x_plane = keep.tile([P, PASSES, TOKENS], U8, name="x_plane", align_bytes=64)
         planes = []
         for s in range(PASSES // 2):
@@ -50,18 +55,19 @@ def tile_causalselfattention_pa_kernel(tc, x_words, x_scales, W_qk_words, W_qk_s
         bias_all = keep.tile([P, COLS], BF16, name="bias_all")
         bias_rows = keep.tile([P, BANK], BF16, name="bias_rows")
         ident = keep.tile([P, P], BF16, name="ident")
-        cos_t = keep.tile([P, BANK], F32, name="cos_t")
-        sin_t = keep.tile([P, BANK], F32, name="sin_t")
-        col_i = keep.tile([P, HALF], I32, name="col_i")
+        ident_f = keep.tile([P, P], F32, name="ident_f")
         row_i = keep.tile([P, 1], I32, name="row_i")
+        pos_i = scr_i[:, 2 * HALF:3 * HALF]
+        tab = ptab.tile([P, BANK], F32, name="tab")
 
         nc.vector.memset(planes[0][:].bitcast(I32), 0)
         nc.vector.memset(planes[1][:].bitcast(I32), 0)
-        nc.vector.memset(xs_raw[:].bitcast(I32), 0)
+        nc.vector.memset(xs_raw.bitcast(I32), 0)
         nc.gpsimd.memset(bias_rows[:], 0.0)
-        nc.gpsimd.iota(col_i[:], pattern=[[1, HALF]], base=0, channel_multiplier=0)
+        nc.gpsimd.iota(pos_i, pattern=[[1, TOKENS // 2], [0, 2]], base=0, channel_multiplier=0)
         nc.gpsimd.iota(row_i[:], pattern=[[0, 1]], base=0, channel_multiplier=1)
         make_identity(nc, ident[:])
+        make_identity(nc, ident_f[:])
         for s in range(2, PASSES // 2):
             nc.gpsimd.memset(planes[s][:].bitcast(F32), 0.0)
 
@@ -101,7 +107,7 @@ def tile_causalselfattention_pa_kernel(tc, x_words, x_scales, W_qk_words, W_qk_s
                     chunk_tiles[(c, k * ng + i)] = (t, i)
 
         nc.scalar.dma_start(out=bias_rows[0:16, :], in_=b_qk.rearrange("(n c) -> n c", c=BANK))
-        nc.sync.dma_start(out=x_raw[:].bitcast(I32), in_=x_words.rearrange("g p n -> p g n").bitcast(I32))
+        nc.sync.dma_start(out=x_raw.bitcast(I32), in_=x_words.rearrange("g p n -> p g n").bitcast(I32))
         load_group_scales(0)
         load_group_scales(1)
         load_group_scales(2)
@@ -111,14 +117,12 @@ def tile_causalselfattention_pa_kernel(tc, x_words, x_scales, W_qk_words, W_qk_s
         load_codes(1, 0, 8)
         load_codes(2, 0, 8)
 
-        col_f = keep.tile([P, HALF], F32, name="col_f")
-        nc.vector.tensor_copy(out=col_f[:], in_=col_i[:])
-        pos_i = keep.tile([P, 1], I32, name="pos_i")
-        nc.vector.tensor_single_scalar(out=pos_i[:], in_=row_i[:], scalar=1, op=ALU.arith_shift_right)
-        pos_f = keep.tile([P, 1], F32, name="pos_f")
-        nc.vector.tensor_copy(out=pos_f[:], in_=pos_i[:])
-        freq = keep.tile([P, HALF], F32, name="freq")
-        nc.scalar.activation(out=freq[:], in_=col_f[:], func=ACT.Exp, scale=-LN_ROPE_BASE / HALF)
+        pos_f = scr_f[:, 6 * HALF:7 * HALF]
+        nc.vector.tensor_copy(out=pos_f, in_=pos_i)
+        row_f = keep.tile([P, 1], F32, name="row_f")
+        nc.vector.tensor_copy(out=row_f[:], in_=row_i[:])
+        freq = keep.tile([P, 1], F32, name="freq")
+        nc.scalar.activation(out=freq[:], in_=row_f[:], func=ACT.Exp, scale=-LN_ROPE_BASE / HALF)
 
         for g in range(PASSES):
             nc.vector.tensor_copy(
@@ -126,16 +130,16 @@ def tile_causalselfattention_pa_kernel(tc, x_words, x_scales, W_qk_words, W_qk_s
                 in_=x_raw[:, g, :].rearrange("p (b t e) -> p t b e", b=2, e=2),
             )
 
-        ang = keep.tile([P, 2 * HALF], F32, name="ang")
-        nc.vector.tensor_scalar(out=ang[:, 0:HALF], in0=freq[:], scalar1=pos_f[:, 0:1], scalar2=None, op0=ALU.mult)
-        nc.vector.tensor_scalar(out=ang[:, HALF:2 * HALF], in0=freq[:], scalar1=pos_f[:, 0:1], scalar2=0.5 * PI, op0=ALU.mult, op1=ALU.add)
-        turns_i = keep.tile([P, 2 * HALF], I32, name="turns_i")
+        ang = scr_f[:, 0:2 * HALF]
+        nc.vector.tensor_scalar(out=ang[:, 0:HALF], in0=pos_f, scalar1=freq[:, 0:1], scalar2=None, op0=ALU.mult)
+        nc.vector.tensor_scalar(out=ang[:, HALF:2 * HALF], in0=pos_f, scalar1=freq[:, 0:1], scalar2=0.5 * PI, op0=ALU.mult, op1=ALU.add)
+        turns_i = scr_i[:, 0:2 * HALF]
         nc.vector.tensor_scalar(out=turns_i[:], in0=ang[:], scalar1=0.5 / PI, scalar2=None, op0=ALU.mult)
-        turns = keep.tile([P, 2 * HALF], F32, name="turns")
+        turns = scr_f[:, 2 * HALF:4 * HALF]
         nc.vector.tensor_copy(out=turns[:], in_=turns_i[:])
         big = 6.28125
         small = 2.0 * PI - big
-        flag = keep.tile([P, 2 * HALF], F32, name="flag")
+        flag = scr_f[:, 4 * HALF:6 * HALF]
         nc.vector.scalar_tensor_tensor(out=ang[:], in0=turns[:], scalar=-big, in1=ang[:], op0=ALU.mult, op1=ALU.add)
         nc.vector.scalar_tensor_tensor(out=ang[:], in0=turns[:], scalar=-small, in1=ang[:], op0=ALU.mult, op1=ALU.add)
         nc.vector.tensor_scalar(out=flag[:], in0=ang[:], scalar1=PI, scalar2=None, op0=ALU.is_gt)
@@ -145,7 +149,7 @@ def tile_causalselfattention_pa_kernel(tc, x_words, x_scales, W_qk_words, W_qk_s
 
         nc.vector.tensor_copy(
             out=x_plane[:].rearrange("p g (t b) -> p g t b", b=2),
-            in_=xs_raw[:].rearrange("p g (b t) -> p g t b", b=2),
+            in_=xs_raw.rearrange("p g (b t) -> p g t b", b=2),
         )
 
         for n in range(COLS // BANK):
@@ -153,9 +157,14 @@ def tile_causalselfattention_pa_kernel(tc, x_words, x_scales, W_qk_words, W_qk_s
             nc.tensor.matmul(out=pb[:], lhsT=ident[:, n:n + 1].to_broadcast([P, P]), rhs=bias_rows[:], start=True, stop=True)
             nc.scalar.copy(out=bias_all[:, n * BANK:(n + 1) * BANK], in_=pb[:])
 
-        for i in range(4):
-            nc.scalar.activation(out=cos_t[:, i * HALF:(i + 1) * HALF], in_=ang[:, HALF:2 * HALF], func=ACT.Sin)
-            nc.scalar.activation(out=sin_t[:, i * HALF:(i + 1) * HALF], in_=ang[:, 0:HALF], func=ACT.Sin, scale=(1.0 if i % 2 == 0 else -1.0))
+        nc.scalar.activation(out=scr_t[:, 0:HALF], in_=ang[:, HALF:2 * HALF], func=ACT.Sin)
+        nc.scalar.activation(out=scr_t[:, HALF:2 * HALF], in_=ang[:, 0:HALF], func=ACT.Sin)
+        nc.scalar.activation(out=scr_t[:, 2 * HALF:3 * HALF], in_=ang[:, 0:HALF], func=ACT.Sin, scale=-1.0)
+        for i in range(3):
+            nc.tensor.transpose(tab[:, i * HALF:(i + 1) * HALF], scr_t[:, i * HALF:(i + 1) * HALF], ident_f[:])
+
+        def table(i, n):
+            return tab[:, i * HALF:(i + 1) * HALF].unsqueeze(1).to_broadcast([P, n, HALF])
 
         def multiply(c):
             nb = CHUNK_BANKS[c]
@@ -179,23 +188,27 @@ def tile_causalselfattention_pa_kernel(tc, x_words, x_scales, W_qk_words, W_qk_s
             return accs
 
         def rotate(parts):
-            vs = []
-            for acc, col in parts:
-                v = work.tile([P, BANK], F32, name="v", tag="v")
-                nc.vector.tensor_tensor(out=v[:], in0=acc[:], in1=bias_all[:, col:col + BANK], op=ALU.add)
-                vs.append(v)
-            prods = []
-            for v in vs:
+            u = work.tile([P, 2 * BANK], F32, name="u", tag="u")
+            bsw = work.tile([P, 2 * BANK], F32, name="bsw", tag="bsw")
+            outs = []
+            for k, (acc, col) in enumerate(parts):
+                nc.vector.tensor_tensor(out=u[:, k * BANK:(k + 1) * BANK], in0=acc[:], in1=bias_all[:, col:col + BANK], op=ALU.add)
+            for k, (acc, col) in enumerate(parts):
                 a = outp.tile([P, BANK], F32, name="a", tag="a")
-                b = work.tile([P, BANK], F32, name="b", tag="b")
-                nc.vector.tensor_tensor(out=a[:], in0=v[:], in1=cos_t[:], op=ALU.mult)
-                nc.vector.tensor_tensor(out=b[:], in0=v[:], in1=sin_t[:], op=ALU.mult)
-                prods.append((a, b))
-            for (acc, col), (a, b) in zip(parts, prods):
-                a4 = a[:].rearrange("p (h s j) -> p h s j", s=2, j=HALF)
-                b4 = b[:].rearrange("p (h s j) -> p h s j", s=2, j=HALF)
-                nc.vector.tensor_tensor(out=a4[:, :, 0, :], in0=a4[:, :, 0, :], in1=b4[:, :, 1, :], op=ALU.add)
-                nc.vector.tensor_tensor(out=a4[:, :, 1, :], in0=a4[:, :, 1, :], in1=b4[:, :, 0, :], op=ALU.add)
+                nc.vector.tensor_tensor(
+                    out=a[:].rearrange("p (n j) -> p n j", j=HALF),
+                    in0=u[:, k * BANK:(k + 1) * BANK].rearrange("p (n j) -> p n j", j=HALF),
+                    in1=table(0, BANK // HALF),
+                    op=ALU.mult,
+                )
+                outs.append(a)
+            u4 = u[:].rearrange("p (h s j) -> p h s j", s=2, j=HALF)
+            b4 = bsw[:].rearrange("p (h s j) -> p h s j", s=2, j=HALF)
+            nc.vector.tensor_tensor(out=b4[:, :, 0, :], in0=u4[:, :, 1, :], in1=table(2, 2 * BANK // HEAD_DIM), op=ALU.mult)
+            nc.vector.tensor_tensor(out=b4[:, :, 1, :], in0=u4[:, :, 0, :], in1=table(1, 2 * BANK // HEAD_DIM), op=ALU.mult)
+            for k, (acc, col) in enumerate(parts):
+                a = outs[k]
+                nc.gpsimd.tensor_tensor(out=a[:], in0=a[:], in1=bsw[:, k * BANK:(k + 1) * BANK], op=ALU.add)
                 for hh in range(BANK // HEAD_DIM):
                     head = col // HEAD_DIM + hh
                     dst = out_0 if head < HEADS else out_1

@@ -45,7 +45,8 @@ def tile_causalselfattention_pa_kernel(tc, x_words, x_scales, W_qk_words, W_qk_s
         scr_t = work.tile([P, 2 * BANK], F32, name="scr_t", tag="bsw")
         scr_x = work.tile([P, 8 * BANK], U8, name="scr_x", tag="bsw")
         x_raw = scr_x[:, 0:PASSES * 2 * TOKENS].rearrange("p (g n) -> p g n", g=PASSES)
-        xs_raw = scr_x[:, PASSES * 2 * TOKENS:PASSES * 3 * TOKENS].rearrange("p (g n) -> p g n", g=PASSES)
+        xs_tile = keep.tile([P, PASSES, TOKENS], U8, name="xs_raw")
+        xs_raw = xs_tile[:]
         x_codes = keep.tile([P, PASSES, 2 * TOKENS], U8, name="x_codes", align_bytes=64)
         x_plane = keep.tile([P, PASSES, TOKENS], U8, name="x_plane", align_bytes=64)
         planes = []

@@ -61,9 +61,9 @@ def tile_causalselfattention_pa_kernel(tc, x_words, x_scales, W_qk_words, W_qk_s
         pos_i = scr_i[:, 2 * HALF:3 * HALF]
         tab = ptab.tile([P, BANK], F32, name="tab")
 
+        nc.vector.memset(xs_raw.bitcast(I32), 0)
         nc.vector.memset(planes[0][:].bitcast(I32), 0)
         nc.vector.memset(planes[1][:].bitcast(I32), 0)
-        nc.vector.memset(xs_raw.bitcast(I32), 0)
         nc.gpsimd.memset(bias_rows[:], 0.0)
         nc.gpsimd.iota(pos_i, pattern=[[1, TOKENS // 2], [0, 2]], base=0, channel_multiplier=0)
         nc.gpsimd.iota(row_i[:], pattern=[[0, 1]], base=0, channel_multiplier=1)
@@ -109,12 +109,12 @@ def tile_causalselfattention_pa_kernel(tc, x_words, x_scales, W_qk_words, W_qk_s
 
         nc.scalar.dma_start(out=bias_rows[0:16, :], in_=b_qk.rearrange("(n c) -> n c", c=BANK))
         nc.sync.dma_start(out=x_raw.bitcast(I32), in_=x_words.rearrange("g p n -> p g n").bitcast(I32))
+        load_scale_rows(xs_raw, x_scales)
+        load_codes(0, 0, 8)
         load_group_scales(0)
         load_group_scales(1)
         load_group_scales(2)
         load_group_scales(3)
-        load_scale_rows(xs_raw, x_scales)
-        load_codes(0, 0, 8)
         load_codes(1, 0, 8)
         load_codes(2, 0, 8)
 

@@ -188,7 +188,7 @@ def tile_causalselfattention_pa_kernel(tc, x_words, x_scales, W_qk_words, W_qk_s
                     )
             return accs
 
-        def rotate(parts):
+        def rotate(parts, adder):
             u = work.tile([P, 2 * BANK], F32, name="u", tag="u")
             bsw = work.tile([P, 2 * BANK], F32, name="bsw", tag="bsw")
             outs = []
@@ -209,7 +209,7 @@ def tile_causalselfattention_pa_kernel(tc, x_words, x_scales, W_qk_words, W_qk_s
             nc.vector.tensor_tensor(out=b4[:, :, 1, :], in0=u4[:, :, 0, :], in1=table(1, 2 * BANK // HEAD_DIM), op=ALU.mult)
             for k, (acc, col) in enumerate(parts):
                 a = outs[k]
-                nc.gpsimd.tensor_tensor(out=a[:], in0=a[:], in1=bsw[:, k * BANK:(k + 1) * BANK], op=ALU.add)
+                adder.tensor_tensor(out=a[:], in0=a[:], in1=bsw[:, k * BANK:(k + 1) * BANK], op=ALU.add)
                 for hh in range(BANK // HEAD_DIM):
                     head = col // HEAD_DIM + hh
                     dst = out_0 if head < HEADS else out_1
@@ -224,4 +224,5 @@ def tile_causalselfattention_pa_kernel(tc, x_words, x_scales, W_qk_words, W_qk_s
                 for k in range(RESIDENT_CHUNKS, len(CHUNK_BANKS)):
                     load_codes(k, 0, PASSES * CHUNK_BANKS[k] // 4)
             for j in range(0, CHUNK_BANKS[c], 2):
-                rotate([(accs[j], starts[c] + j * BANK), (accs[j + 1], starts[c] + (j + 1) * BANK)])
+                adder = nc.vector if c == len(CHUNK_BANKS) - 1 else nc.gpsimd
+                rotate([(accs[j], starts[c] + j * BANK), (accs[j + 1], starts[c] + (j + 1) * BANK)], adder)

@@ -27,6 +27,7 @@ FLOPS = 2 * TOKENS * 4096 * COLS
 
 CHUNK_BANKS = [4, 4, 4, 2, 2]
 RESIDENT_CHUNKS = 3
+LATE_PASS = 6
 
 
 def tile_causalselfattention_pa_kernel(tc, x_words, x_scales, W_qk_words, W_qk_scales, b_qk, out_0, out_1):
@@ -45,8 +46,8 @@ def tile_causalselfattention_pa_kernel(tc, x_words, x_scales, W_qk_words, W_qk_s
         scr_t = work.tile([P, 2 * BANK], F32, name="scr_t", tag="bsw")
         scr_x = work.tile([P, 8 * BANK], U8, name="scr_x", tag="bsw")
         x_raw = scr_x[:, 0:PASSES * 2 * TOKENS].rearrange("p (g n) -> p g n", g=PASSES)
-        xs_tile = keep.tile([P, PASSES, TOKENS], U8, name="xs_raw")
-        xs_raw = xs_tile[:]
+        xs_early = keep.tile([P, LATE_PASS, TOKENS], U8, name="xs_early")
+        xs_late = keep.tile([P, PASSES - LATE_PASS, TOKENS], U8, name="xs_late")
         x_codes = keep.tile([P, PASSES, 2 * TOKENS], U8, name="x_codes", align_bytes=64)
         x_plane = keep.tile([P, PASSES, TOKENS], U8, name="x_plane", align_bytes=64)
         planes = []
@@ -61,7 +62,8 @@ def tile_causalselfattention_pa_kernel(tc, x_words, x_scales, W_qk_words, W_qk_s
         pos_i = scr_i[:, 2 * HALF:3 * HALF]
         tab = ptab.tile([P, BANK], F32, name="tab")
 
-        nc.vector.memset(xs_raw.bitcast(I32), 0)
+        nc.vector.memset(xs_early[:].bitcast(I32), 0)
+        nc.vector.memset(xs_late[:].bitcast(I32), 0)
         nc.vector.memset(planes[0][:].bitcast(I32), 0)
         nc.vector.memset(planes[1][:].bitcast(I32), 0)
         nc.gpsimd.memset(bias_rows[:], 0.0)
@@ -109,12 +111,13 @@ def tile_causalselfattention_pa_kernel(tc, x_words, x_scales, W_qk_words, W_qk_s
 
         nc.scalar.dma_start(out=bias_rows[0:16, :], in_=b_qk.rearrange("(n c) -> n c", c=BANK))
         nc.sync.dma_start(out=x_raw.bitcast(I32), in_=x_words.rearrange("g p n -> p g n").bitcast(I32))
-        load_scale_rows(xs_raw, x_scales)
+        load_scale_rows(xs_early, x_scales[0:LATE_PASS])
         load_codes(0, 0, 8)
         load_group_scales(0)
         load_group_scales(1)
         load_group_scales(2)
         load_group_scales(3)
+        load_scale_rows(xs_late, x_scales[LATE_PASS:PASSES])
         load_codes(1, 0, 8)
         load_codes(2, 0, 8)
 
@@ -149,8 +152,12 @@ def tile_causalselfattention_pa_kernel(tc, x_words, x_scales, W_qk_words, W_qk_s
         nc.vector.scalar_tensor_tensor(out=ang[:], in0=flag[:], scalar=2.0 * PI, in1=ang[:], op0=ALU.mult, op1=ALU.add)
 
         nc.vector.tensor_copy(
-            out=x_plane[:].rearrange("p g (t b) -> p g t b", b=2),
-            in_=xs_raw.rearrange("p g (b t) -> p g t b", b=2),
+            out=x_plane[:, 0:LATE_PASS, :].rearrange("p g (t b) -> p g t b", b=2),
+            in_=xs_early[:].rearrange("p g (b t) -> p g t b", b=2),
+        )
+        nc.vector.tensor_copy(
+            out=x_plane[:, LATE_PASS:PASSES, :].rearrange("p g (t b) -> p g t b", b=2),
+            in_=xs_late[:].rearrange("p g (b t) -> p g t b", b=2),
         )
 
         for n in range(COLS // BANK):

@@ -27,6 +27,7 @@ FLOPS = 2 * TOKENS * 4096 * COLS
 
 CHUNK_BANKS = [4, 4, 4, 2, 2]
 RESIDENT_CHUNKS = 3
+PLANE_PASSES = [4, 2, 2]
 LATE_PASS = 6
 
 
@@ -51,9 +52,12 @@ def tile_causalselfattention_pa_kernel(tc, x_words, x_scales, W_qk_words, W_qk_s
         x_codes = keep.tile([P, PASSES, 2 * TOKENS], U8, name="x_codes", align_bytes=64)
         x_plane = keep.tile([P, PASSES, TOKENS], U8, name="x_plane", align_bytes=64)
         planes = []
-        for s in range(PASSES // 2):
-            pl = keep.tile([P, 2, COLS], U8, name="plane%d" % s, align_bytes=64)
+        plane_of = []
+        for i, n in enumerate(PLANE_PASSES):
+            pl = keep.tile([P, n, COLS], U8, name="plane%d" % i, align_bytes=64)
             planes.append(pl)
+            for k in range(n):
+                plane_of.append((pl, k))
         bias_all = keep.tile([P, COLS], BF16, name="bias_all")
         bias_rows = keep.tile([P, BANK], BF16, name="bias_rows")
         ident = keep.tile([P, P], BF16, name="ident")
@@ -65,14 +69,13 @@ def tile_causalselfattention_pa_kernel(tc, x_words, x_scales, W_qk_words, W_qk_s
         nc.vector.memset(xs_early[:].bitcast(I32), 0)
         nc.vector.memset(xs_late[:].bitcast(I32), 0)
         nc.vector.memset(planes[0][:].bitcast(I32), 0)
-        nc.vector.memset(planes[1][:].bitcast(I32), 0)
         nc.gpsimd.memset(bias_rows[:], 0.0)
         nc.gpsimd.iota(pos_i, pattern=[[1, TOKENS // 2], [0, 2]], base=0, channel_multiplier=0)
         nc.gpsimd.iota(row_i[:], pattern=[[0, 1]], base=0, channel_multiplier=1)
         make_identity(nc, ident[:])
         make_identity(nc, ident_f[:])
-        for s in range(2, PASSES // 2):
-            nc.gpsimd.memset(planes[s][:].bitcast(F32), 0.0)
+        for i in range(1, len(PLANE_PASSES)):
+            nc.gpsimd.memset(planes[i][:].bitcast(F32), 0.0)
 
         def load_scale_rows(plane, src):
             for r in range(4):
@@ -81,12 +84,13 @@ def tile_causalselfattention_pa_kernel(tc, x_words, x_scales, W_qk_words, W_qk_s
                     in_=src[:, r:16:4, :].rearrange("g q n -> q g n").bitcast(I32),
                 )
 
-        def load_group_scales(s):
+        def load_group_scales(i):
+            g0 = sum(PLANE_PASSES[:i])
             for p in (0, 1, 2, 3, 32, 33, 34, 35):
                 q = 4 * (p // 32) + p % 32
                 nc.sync.dma_start(
-                    out=planes[s][p:P:64, :, :].bitcast(I32),
-                    in_=W_qk_scales[2 * s:2 * s + 2, q:16:8, :].rearrange("g q n -> q g n").bitcast(I32),
+                    out=planes[i][p:P:64, :, :].bitcast(I32),
+                    in_=W_qk_scales[g0:g0 + PLANE_PASSES[i], q:16:8, :].rearrange("g q n -> q g n").bitcast(I32),
                 )
 
         starts = []
@@ -113,10 +117,8 @@ def tile_causalselfattention_pa_kernel(tc, x_words, x_scales, W_qk_words, W_qk_s
         nc.sync.dma_start(out=x_raw.bitcast(I32), in_=x_words.rearrange("g p n -> p g n").bitcast(I32))
         load_scale_rows(xs_early, x_scales[0:LATE_PASS])
         load_codes(0, 0, 8)
-        load_group_scales(0)
-        load_group_scales(1)
-        load_group_scales(2)
-        load_group_scales(3)
+        for i in range(len(PLANE_PASSES)):
+            load_group_scales(i)
         load_scale_rows(xs_late, x_scales[LATE_PASS:PASSES])
         load_codes(1, 0, 8)
         load_codes(2, 0, 8)
@@ -189,7 +191,7 @@ def tile_causalselfattention_pa_kernel(tc, x_words, x_scales, W_qk_words, W_qk_s
                         lhsT=x_codes[:, g, :].bitcast(FP4X4),
                         lhsT_scale=x_plane[:, g, :],
                         rhs=t[:, i, j * 2 * BANK:(j + 1) * 2 * BANK].bitcast(FP4X4),
-                        rhs_scale=planes[g // 2][:, g % 2, off + j * BANK:off + (j + 1) * BANK],
+                        rhs_scale=plane_of[g][0][:, plane_of[g][1], off + j * BANK:off + (j + 1) * BANK],
                         start=(g == 0),
                         stop=(g == PASSES - 1),
                     )

from contextlib import ExitStack

import concourse.mybir as mybir
from concourse.masks import make_identity

F32 = mybir.dt.float32
BF16 = mybir.dt.bfloat16
I32 = mybir.dt.int32
U8 = mybir.dt.uint8
FP4X4 = mybir.dt.float4_e2m1fn_x4
ALU = mybir.AluOpType
ACT = mybir.ActivationFunctionType

P = 128
PASSES = 8
TOKENS = 128
HEADS = 16
HEAD_DIM = 256
HALF = 128
COLS = 8192
BANK = 512
GROUP_COLS = 2048
LN_ROPE_BASE = 9.210340371976184
PI = 3.141592653589793

FLOPS = 2 * TOKENS * 4096 * COLS

CHUNK_BANKS = [4, 4, 4, 2, 2]
RESIDENT_CHUNKS = 3
PLANE_PASSES = [4, 2, 2]
LATE_PASS = 6


def tile_causalselfattention_pa_kernel(tc, x_words, x_scales, W_qk_words, W_qk_scales, b_qk, out_0, out_1):
    nc = tc.nc
    with ExitStack() as ctx:
        keep = ctx.enter_context(tc.tile_pool(name="keep", bufs=1))
        wpool = ctx.enter_context(tc.tile_pool(name="wpool", bufs=24))
        work = ctx.enter_context(tc.tile_pool(name="work", bufs=2))
        outp = ctx.enter_context(tc.tile_pool(name="outp", bufs=16))
        ptab = ctx.enter_context(tc.psum_pool(name="ptab", bufs=1))
        psum = ctx.enter_context(tc.psum_pool(name="psum", bufs=7))
        ctx.enter_context(tc.manual_schedule())

        scr_f = work.tile([P, 2 * BANK], F32, name="scr_f", tag="u")
        scr_i = work.tile([P, 2 * BANK], I32, name="scr_i", tag="u")
        scr_t = work.tile([P, 2 * BANK], F32, name="scr_t", tag="bsw")
        scr_x = work.tile([P, 8 * BANK], U8, name="scr_x", tag="bsw")
        x_raw = scr_x[:, 0:PASSES * 2 * TOKENS].rearrange("p (g n) -> p g n", g=PASSES)
        xs_early = keep.tile([P, LATE_PASS, TOKENS], U8, name="xs_early")
        xs_late = keep.tile([P, PASSES - LATE_PASS, TOKENS], U8, name="xs_late")
        x_codes = keep.tile([P, PASSES, 2 * TOKENS], U8, name="x_codes", align_bytes=64)
        x_plane = keep.tile([P, PASSES, TOKENS], U8, name="x_plane", align_bytes=64)
        planes = []
        plane_of = []
        for i, n in enumerate(PLANE_PASSES):
            pl = keep.tile([P, n, COLS], U8, name="plane%d" % i, align_bytes=64)
            planes.append(pl)
            for k in range(n):
                plane_of.append((pl, k))
        bias_all = keep.tile([P, COLS], BF16, name="bias_all")
        bias_rows = keep.tile([P, BANK], BF16, name="bias_rows")
        ident = keep.tile([P, P], BF16, name="ident")
        ident_f = keep.tile([P, P], F32, name="ident_f")
        row_i = keep.tile([P, 1], I32, name="row_i")
        pos_i = scr_i[:, 2 * HALF:3 * HALF]
        tab = ptab.tile([P, BANK], F32, name="tab")

        nc.vector.memset(xs_early[:].bitcast(I32), 0)
        nc.vector.memset(xs_late[:].bitcast(I32), 0)
        nc.vector.memset(planes[0][:].bitcast(I32), 0)
        nc.gpsimd.memset(bias_rows[:], 0.0)
        nc.gpsimd.iota(pos_i, pattern=[[1, TOKENS // 2], [0, 2]], base=0, channel_multiplier=0)
        nc.gpsimd.iota(row_i[:], pattern=[[0, 1]], base=0, channel_multiplier=1)
        make_identity(nc, ident[:])
        make_identity(nc, ident_f[:])
        for i in range(1, len(PLANE_PASSES)):
            nc.gpsimd.memset(planes[i][:].bitcast(F32), 0.0)

        def load_scale_rows(plane, src):
            for r in range(4):
                nc.sync.dma_start(
                    out=plane[r:P:32, :, :].bitcast(I32),
                    in_=src[:, r:16:4, :].rearrange("g q n -> q g n").bitcast(I32),
                )

        def load_group_scales(i):
            g0 = sum(PLANE_PASSES[:i])
            for p in (0, 1, 2, 3, 32, 33, 34, 35):
                q = 4 * (p // 32) + p % 32
                nc.sync.dma_start(
                    out=planes[i][p:P:64, :, :].bitcast(I32),
                    in_=W_qk_scales[g0:g0 + PLANE_PASSES[i], q:16:8, :].rearrange("g q n -> q g n").bitcast(I32),
                )

        starts = []
        c0 = 0
        for nb in CHUNK_BANKS:
            starts.append(c0)
            c0 += nb * BANK

        chunk_tiles = {}

        def load_codes(c, first, count):
            nb = CHUNK_BANKS[c]
            ng = 4 // nb
            for k in range(first, first + count):
                t = wpool.tile([P, ng, nb * 2 * BANK], U8, name="wc", tag="wc", align_bytes=64)
                nc.sync.dma_start(
                    out=t[:].bitcast(I32),
                    in_=W_qk_words[k * ng:(k + 1) * ng, :, 2 * starts[c]:2 * (starts[c] + nb * BANK)].rearrange("g p n -> p g n").bitcast(I32),
                )
                for i in range(ng):
                    chunk_tiles[(c, k * ng + i)] = (t, i)

        nc.scalar.dma_start(out=bias_rows[0:16, :], in_=b_qk.rearrange("(n c) -> n c", c=BANK))
        nc.sync.dma_start(out=x_raw.bitcast(I32), in_=x_words.rearrange("g p n -> p g n").bitcast(I32))
        load_scale_rows(xs_early, x_scales[0:LATE_PASS])
        load_codes(0, 0, 8)
        for i in range(len(PLANE_PASSES)):
            load_group_scales(i)
        load_scale_rows(xs_late, x_scales[LATE_PASS:PASSES])
        load_codes(1, 0, 8)
        load_codes(2, 0, 8)

        pos_f = scr_f[:, 6 * HALF:7 * HALF]
        nc.vector.tensor_copy(out=pos_f, in_=pos_i)
        row_f = keep.tile([P, 1], F32, name="row_f")
        nc.vector.tensor_copy(out=row_f[:], in_=row_i[:])
        freq = keep.tile([P, 1], F32, name="freq")
        nc.scalar.activation(out=freq[:], in_=row_f[:], func=ACT.Exp, scale=-LN_ROPE_BASE / HALF)

        for g in range(PASSES):
            nc.vector.tensor_copy(
                out=x_codes[:, g, :].rearrange("p (t b e) -> p t b e", b=2, e=2),
                in_=x_raw[:, g, :].rearrange("p (b t e) -> p t b e", b=2, e=2),
            )

        ang = scr_f[:, 0:2 * HALF]
        nc.vector.tensor_scalar(out=ang[:, 0:HALF], in0=pos_f, scalar1=freq[:, 0:1], scalar2=None, op0=ALU.mult)
        nc.vector.tensor_scalar(out=ang[:, HALF:2 * HALF], in0=pos_f, scalar1=freq[:, 0:1], scalar2=0.5 * PI, op0=ALU.mult, op1=ALU.add)
        turns_i = scr_i[:, 0:2 * HALF]
        nc.vector.tensor_scalar(out=turns_i[:], in0=ang[:], scalar1=0.5 / PI, scalar2=None, op0=ALU.mult)
        turns = scr_f[:, 2 * HALF:4 * HALF]
        nc.vector.tensor_copy(out=turns[:], in_=turns_i[:])
        big = 6.28125
        small = 2.0 * PI - big
        flag = scr_f[:, 4 * HALF:6 * HALF]
        nc.vector.scalar_tensor_tensor(out=ang[:], in0=turns[:], scalar=-big, in1=ang[:], op0=ALU.mult, op1=ALU.add)
        nc.vector.scalar_tensor_tensor(out=ang[:], in0=turns[:], scalar=-small, in1=ang[:], op0=ALU.mult, op1=ALU.add)
        nc.vector.tensor_scalar(out=flag[:], in0=ang[:], scalar1=PI, scalar2=None, op0=ALU.is_gt)
        nc.vector.scalar_tensor_tensor(out=ang[:], in0=flag[:], scalar=-2.0 * PI, in1=ang[:], op0=ALU.mult, op1=ALU.add)
        nc.vector.tensor_scalar(out=flag[:], in0=ang[:], scalar1=-PI, scalar2=None, op0=ALU.is_lt)
        nc.vector.scalar_tensor_tensor(out=ang[:], in0=flag[:], scalar=2.0 * PI, in1=ang[:], op0=ALU.mult, op1=ALU.add)

        nc.vector.tensor_copy(
            out=x_plane[:, 0:LATE_PASS, :].rearrange("p g (t b) -> p g t b", b=2),
            in_=xs_early[:].rearrange("p g (b t) -> p g t b", b=2),
        )
        nc.vector.tensor_copy(
            out=x_plane[:, LATE_PASS:PASSES, :].rearrange("p g (t b) -> p g t b", b=2),
            in_=xs_late[:].rearrange("p g (b t) -> p g t b", b=2),
        )

        for n in range(COLS // BANK):
            pb = psum.tile([P, BANK], F32, name="acc", tag="acc")
            nc.tensor.matmul(out=pb[:], lhsT=ident[:, n:n + 1].to_broadcast([P, P]), rhs=bias_rows[:], start=True, stop=True)
            nc.scalar.copy(out=bias_all[:, n * BANK:(n + 1) * BANK], in_=pb[:])

        nc.scalar.activation(out=scr_t[:, 0:HALF], in_=ang[:, HALF:2 * HALF], func=ACT.Sin)
        nc.scalar.activation(out=scr_t[:, HALF:2 * HALF], in_=ang[:, 0:HALF], func=ACT.Sin)
        nc.scalar.activation(out=scr_t[:, 2 * HALF:3 * HALF], in_=ang[:, 0:HALF], func=ACT.Sin, scale=-1.0)
        for i in range(3):
            nc.tensor.transpose(tab[:, i * HALF:(i + 1) * HALF], scr_t[:, i * HALF:(i + 1) * HALF], ident_f[:])

        def table(i, n):
            return tab[:, i * HALF:(i + 1) * HALF].unsqueeze(1).to_broadcast([P, n, HALF])

        def multiply(c):
            nb = CHUNK_BANKS[c]
            accs = []
            for j in range(nb):
                acc = psum.tile([P, BANK], F32, name="acc", tag="acc")
                accs.append(acc)
            off = starts[c]
            for g in range(PASSES):
                t, i = chunk_tiles[(c, g)]
                for j in range(nb):
                    nc.tensor.matmul_mx(
                        out=accs[j][:],
                        lhsT=x_codes[:, g, :].bitcast(FP4X4),
                        lhsT_scale=x_plane[:, g, :],
                        rhs=t[:, i, j * 2 * BANK:(j + 1) * 2 * BANK].bitcast(FP4X4),
                        rhs_scale=plane_of[g][0][:, plane_of[g][1], off + j * BANK:off + (j + 1) * BANK],
                        start=(g == 0),
                        stop=(g == PASSES - 1),
                    )
            return accs

        def rotate(parts, adder):
            u = work.tile([P, 2 * BANK], F32, name="u", tag="u")
            bsw = work.tile([P, 2 * BANK], F32, name="bsw", tag="bsw")
            outs = []
            for k, (acc, col) in enumerate(parts):
                nc.vector.tensor_tensor(out=u[:, k * BANK:(k + 1) * BANK], in0=acc[:], in1=bias_all[:, col:col + BANK], op=ALU.add)
            for k, (acc, col) in enumerate(parts):
                a = outp.tile([P, BANK], F32, name="a", tag="a")
                nc.vector.tensor_tensor(
                    out=a[:].rearrange("p (n j) -> p n j", j=HALF),
                    in0=u[:, k * BANK:(k + 1) * BANK].rearrange("p (n j) -> p n j", j=HALF),
                    in1=table(0, BANK // HALF),
                    op=ALU.mult,
                )
                outs.append(a)
            u4 = u[:].rearrange("p (h s j) -> p h s j", s=2, j=HALF)
            b4 = bsw[:].rearrange("p (h s j) -> p h s j", s=2, j=HALF)
            nc.vector.tensor_tensor(out=b4[:, :, 0, :], in0=u4[:, :, 1, :], in1=table(2, 2 * BANK // HEAD_DIM), op=ALU.mult)
            nc.vector.tensor_tensor(out=b4[:, :, 1, :], in0=u4[:, :, 0, :], in1=table(1, 2 * BANK // HEAD_DIM), op=ALU.mult)
            for k, (acc, col) in enumerate(parts):
                a = outs[k]
                adder.tensor_tensor(out=a[:], in0=a[:], in1=bsw[:, k * BANK:(k + 1) * BANK], op=ALU.add)
                for hh in range(BANK // HEAD_DIM):
                    head = col // HEAD_DIM + hh
                    dst = out_0 if head < HEADS else out_1
                    nc.sync.dma_start(
                        out=dst[:, head % HEADS, :, :].rearrange("b t d -> t b d"),
                        in_=a[:, hh * HEAD_DIM:(hh + 1) * HEAD_DIM],
                    )

        for c in range(len(CHUNK_BANKS)):
            accs = multiply(c)
            if c == 0:
                for k in range(RESIDENT_CHUNKS, len(CHUNK_BANKS)):
                    load_codes(k, 0, PASSES * CHUNK_BANKS[k] // 4)
            for j in range(0, CHUNK_BANKS[c], 2):
                adder = nc.vector if c == len(CHUNK_BANKS) - 1 else nc.gpsimd
                rotate([(accs[j], starts[c] + j * BANK), (accs[j + 1], starts[c] + (j + 1) * BANK)], adder)
